import numpy as np
import ml_dtypes


def mxq(x, axis, fmt="e4m3"):
    dtype, down = {"e4m3": (ml_dtypes.float8_e4m3fn, 7), "e5m2": (ml_dtypes.float8_e5m2, 14)}[fmt]
    v = np.moveaxis(np.asarray(x, np.float32).astype(ml_dtypes.bfloat16).astype(np.float64), axis, -1)
    blocks = v.reshape(v.shape[:-1] + (-1, 32))
    amax = np.abs(blocks).max(-1, keepdims=True)
    byte = np.maximum(np.where(amax > 0, np.frexp(amax)[1] - 1 + 127, 0) - down, 1)
    scale = np.exp2(byte - 127.0)
    codes = (blocks / scale).astype(np.float32).astype(dtype).astype(np.float64)
    return np.moveaxis((codes * scale).reshape(v.shape), -1, axis)


WIDE = False


def mx_kscale(k):
    if not WIDE:
        return np.ones(k)
    levels = np.array([10, -10, 5, -5, 0])
    a = np.random.permutation(np.resize(levels, k // 512 * 4)).reshape(k // 512, 4)
    idx = np.arange(k)
    return np.exp2(a[idx // 512, idx % 128 // 32])


BF16 = ml_dtypes.bfloat16


def bf(x):
    return np.asarray(x, np.float32).astype(BF16)


def f64(x):
    return np.asarray(x).astype(np.float64)


T, H, QR, NH, DN, DR, KVR = 4096, 1024, 512, 2, 128, 64, 64
EPS = 1e-6


def rmsnorm(x, gamma):
    var = np.mean(np.square(x), axis=-1, keepdims=True)
    return x * (1.0 / np.sqrt(var + EPS)) * gamma


def apply_rope(x, cos, sin):
    x1, x2 = np.split(x, 2, axis=-1)
    rot = np.concatenate([-x2, x1], axis=-1)
    return x * cos + rot * sin


def setup_inputs():
    s, t = mx_kscale(H), mx_kscale(QR)
    return {"token_x": bf(np.random.standard_normal((T, H)) * s),
            "wq_a": bf(np.random.standard_normal((H, QR)) / np.sqrt(H) / s[:, None]),
            "wq_b": bf(np.random.standard_normal((QR, NH * (DN + DR))) / np.sqrt(QR) / t[:, None]),
            "wkv": bf(np.random.standard_normal((H, KVR + DR)) / np.sqrt(H) / s[:, None]),
            "rope_cos": bf(np.random.uniform(-1.0, 1.0, (T, DR))),
            "rope_sin": bf(np.random.uniform(-1.0, 1.0, (T, DR))),
            "gamma_cq": bf((1.0 + 0.1 * np.random.standard_normal(QR)) * t),
            "gamma_ckv": bf(1.0 + 0.1 * np.random.standard_normal(KVR))}


def reference(token_x, wq_a, wq_b, wkv, rope_cos, rope_sin, gamma_cq, gamma_ckv):
    cos, sin = f64(rope_cos), f64(rope_sin)
    xq = mxq(f64(token_x), 1, "e4m3")
    cq = rmsnorm(xq @ mxq(f64(wq_a), 0, "e4m3"), f64(gamma_cq))
    q = (mxq(cq, 1, "e4m3") @ mxq(f64(wq_b), 0, "e4m3")).reshape(T, NH, DN + DR)
    q_nope, q_rope = q[..., :DN], q[..., DN:]
    q_rope = apply_rope(q_rope, cos[:, None, :], sin[:, None, :])
    query = np.concatenate([q_nope, q_rope], axis=-1)
    kv = xq @ mxq(f64(wkv), 0, "e4m3")
    ckv = rmsnorm(kv[:, :KVR], f64(gamma_ckv))
    k_rope = apply_rope(kv[:, KVR:], cos, sin)
    return np.concatenate([query.reshape(T, -1), ckv, k_rope], axis=-1)

@@ -1,0 +1,375 @@
+from contextlib import ExitStack
+import math
+
+import concourse.mybir as mybir
+from concourse.masks import make_identity
+
+F32 = mybir.dt.float32
+BF16 = mybir.dt.bfloat16
+U32 = mybir.dt.uint32
+U8 = mybir.dt.uint8
+FP8X4 = mybir.dt.float8_e4m3fn_x4
+ACT = mybir.ActivationFunctionType
+ALU = mybir.AluOpType
+
+T, H, QR, NH, DN, DR, KVR = 4096, 1024, 512, 2, 128, 64, 64
+EPS = 1e-6
+P = 128
+NT = T // P
+CH = 4
+NC = NT // CH
+FLOPS = 2 * T * (H * (QR + KVR + DR) + QR * NH * (DN + DR))
+
+
+def tile_mla_model_t_kernel(
+    tc, token_x, wq_a, wq_b, wkv, rope_cos, rope_sin, gamma_cq, gamma_ckv, out
+):
+    nc = tc.nc
+    with ExitStack() as ctx:
+        const = ctx.enter_context(tc.tile_pool(name="const", bufs=1))
+        ring2 = ctx.enter_context(tc.tile_pool(name="ring2", bufs=2))
+        ring3 = ctx.enter_context(tc.tile_pool(name="ring3", bufs=3))
+        ring6 = ctx.enter_context(tc.tile_pool(name="ring6", bufs=6))
+        psum = ctx.enter_context(tc.psum_pool(name="psum", bufs=2))
+        ctx.enter_context(tc.manual_schedule())
+
+        x_v = token_x.rearrange("(p i) h -> p i h", i=NT)
+        out_v = out.rearrange("(p i) c -> p i c", i=NT)
+
+        wa_raw = const.tile([P, 2, 4, QR], BF16, name="wa_raw")
+        wa_v = wq_a.rearrange("(g u q e) n -> q g u (e n)", g=2, u=2, q=P, e=2)
+        for g in range(2):
+            nc.sync.dma_start(
+                out=wa_raw[:, g].rearrange("q (u e) n -> q u (e n)", u=2), in_=wa_v[:, g]
+            )
+        wk_raw = const.tile([P, 2, 4, P], BF16, name="wk_raw")
+        nc.sync.dma_start(
+            out=wk_raw[:].rearrange("q g (u e) n -> q (g u) (e n)", u=2),
+            in_=wkv.rearrange("(g u q e) n -> q (g u) (e n)", g=2, u=2, q=P, e=2),
+        )
+        gz = const.tile([P, QR + KVR], BF16, name="gz")
+        nc.vector.memset(gz[:], 0.0)
+        nc.sync.dma_start(out=gz[0:1, 0:QR], in_=gamma_cq.rearrange("(o n) -> o n", o=1))
+        nc.sync.dma_start(
+            out=gz[0:1, QR : QR + KVR], in_=gamma_ckv.rearrange("(o n) -> o n", o=1)
+        )
+        x_sb = []
+        for c in range(NC):
+            x_c = const.tile([P, CH, H], BF16, name="x%d" % c)
+            x_sb.append(x_c)
+        nc.sync.dma_start(out=x_sb[0][:, 0:2, :], in_=x_v[:, 0:2, :])
+        nc.sync.dma_start(out=x_sb[0][:, 2:4, :], in_=x_v[:, 2:4, :])
+        wb_raw = const.tile([P, 4, 384], BF16, name="wb_raw")
+        nc.sync.dma_start(out=wb_raw[:], in_=wq_b.rearrange("(t p) n -> p t n", t=4))
+        nc.sync.dma_start(out=x_sb[1][:], in_=x_v[:, CH : 2 * CH, :])
+        cos_sb = const.tile([P, NT, DR], BF16, name="cos_sb")
+        sin_sb = const.tile([P, NT, DR], BF16, name="sin_sb")
+        nc.sync.dma_start(out=cos_sb[:], in_=rope_cos.rearrange("(p i) d -> p i d", i=NT))
+        nc.sync.dma_start(out=sin_sb[:], in_=rope_sin.rearrange("(p i) d -> p i d", i=NT))
+        for c in range(2, NC):
+            nc.sync.dma_start(out=x_sb[c][:], in_=x_v[:, c * CH : (c + 1) * CH, :])
+
+        ident_f = const.tile([P, P], F32, name="ident_f")
+        make_identity(nc, ident_f[:])
+        ident_b = const.tile([P, P], BF16, name="ident_b")
+        make_identity(nc, ident_b[:])
+        ones = const.tile([P, P], BF16, name="ones")
+        nc.vector.memset(ones[:], 1.0)
+        warm = const.tile([P, 1], F32, name="warm")
+        nc.vector.memset(warm[:], 1.0)
+        warm2 = const.tile([P, 1], F32, name="warm2")
+        nc.scalar.activation(out=warm2[:], in_=warm[:], func=ACT.Sqrt)
+        junk = const.tile([P, QR], BF16, name="junk")
+        gam = const.tile([P, QR], F32, name="gam")
+        gamk = const.tile([P, KVR], F32, name="gamk")
+
+        tab = const.tile([P, NT, 2, 2, 32], BF16, name="tab")
+        for c in range(NC):
+            ii = slice(c * CH, (c + 1) * CH)
+            for (xh, yh, src, lo, sign) in (
+                (0, 0, cos_sb, 0, 1.0),
+                (0, 1, sin_sb, 0, -1.0),
+                (1, 0, sin_sb, 32, 1.0),
+                (1, 1, cos_sb, 32, 1.0),
+            ):
+                nc.gpsimd.tensor_scalar(
+                    out=tab[:, ii, xh, yh, :],
+                    in0=src[:, ii, lo : lo + 32],
+                    scalar1=sign,
+                    scalar2=0.0,
+                    op0=ALU.mult,
+                    op1=ALU.add,
+                )
+
+        wa_g = const.tile([P, 2, QR, 4], BF16, name="wa_g", align_bytes=64)
+        wa_c = const.tile([P, 2, QR], U32, name="wa_c", align_bytes=64)
+        wa_s = const.tile([P, 2, QR], U8, name="wa_s", align_bytes=64)
+        for g in range(2):
+            nc.vector.tensor_copy(
+                out=wa_g[:, g].rearrange("p (c i) t -> p c t i", i=4),
+                in_=wa_raw[:, g].rearrange("p t (c i) -> p c t i", i=4),
+            )
+        nc.vector.quantize_mx(
+            out=wa_c[:].rearrange("p g n -> p (g n)").bitcast(FP8X4),
+            scales=wa_s[:].rearrange("p g n -> p (g n)"),
+            in_=wa_g[:].rearrange("p g n t -> p (g n t)"),
+        )
+        wk_g = const.tile([P, 2, P, 4], BF16, name="wk_g", align_bytes=64)
+        wk_c = const.tile([P, 2, P], U32, name="wk_c", align_bytes=64)
+        wk_s = const.tile([P, 2, P], U8, name="wk_s", align_bytes=64)
+        nc.scalar.copy(out=wk_g[:], in_=wk_raw[:].rearrange("p g t n -> p g n t"))
+        wb_g = const.tile([P, 384, 4], BF16, name="wb_g", align_bytes=64)
+        wb_c = const.tile([P, 384], U32, name="wb_c", align_bytes=64)
+        wb_s = const.tile([P, 384], U8, name="wb_s", align_bytes=64)
+
+        def prep_wb_copy():
+            wb_h = wb_raw[:].rearrange("p t (h c) -> p h c t", h=2)
+            nc.scalar.copy(
+                out=wb_g[:, 0:128, :].rearrange("p (h c) t -> p h c t", h=2),
+                in_=wb_h[:, :, 128:192, :],
+            )
+            nc.scalar.copy(
+                out=wb_g[:, 128:384, :].rearrange("p (h c) t -> p h c t", h=2),
+                in_=wb_h[:, :, 0:128, :],
+            )
+
+        def prep_w_quant():
+            nc.vector.quantize_mx(
+                out=wk_c[:].rearrange("p g n -> p (g n)").bitcast(FP8X4),
+                scales=wk_s[:].rearrange("p g n -> p (g n)"),
+                in_=wk_g[:].rearrange("p g n t -> p (g n t)"),
+            )
+            nc.vector.quantize_mx(
+                out=wb_c[:, 0:128].bitcast(FP8X4),
+                scales=wb_s[:, 0:128],
+                in_=wb_g[:, 0:128, :].rearrange("p n t -> p (n t)"),
+            )
+            nc.vector.quantize_mx(
+                out=wb_c[:, 128:384].bitcast(FP8X4),
+                scales=wb_s[:, 128:384],
+                in_=wb_g[:, 128:384, :].rearrange("p n t -> p (n t)"),
+            )
+
+        def prep_gamma_mm():
+            g1 = psum.tile([P, 512], F32, name="ob", tag="ob")
+            nc.tensor.matmul(out=g1[:], lhsT=ones[:], rhs=gz[:, 0:QR], start=True, stop=True)
+            g2 = psum.tile([P, 512], F32, name="ob", tag="ob")
+            nc.tensor.matmul(
+                out=g2[:, 0:KVR], lhsT=ones[:], rhs=gz[:, QR : QR + KVR], start=True, stop=True
+            )
+            nc.scalar.copy(out=gam[:], in_=g1[:])
+            nc.scalar.copy(out=gamk[:], in_=g2[:, 0:KVR])
+
+        XT, XG, XC, XS, A, CQ, CT, CG, CC, CS, OB = {}, {}, {}, {}, {}, {}, {}, {}, {}, {}, {}
+        ST, RA, RK, OC, PR = {}, {}, {}, {}, {}
+
+        def ok(i):
+            return 0 <= i < NT
+
+        def t1(i):
+            xt = psum.tile([P, 4, P], F32, name="xt", tag="xt")
+            xw = x_sb[i // CH][:, i % CH, :].bitcast(F32)
+            for b in range(4):
+                nc.tensor.transpose(xt[:, b, :], xw[:, b * P : (b + 1) * P], ident_f[:])
+            XT[i] = xt
+
+        def c1(i):
+            xg = ring3.tile([P, 2 * P * 4], BF16, name="xg", tag="xg", align_bytes=64)
+            nc.scalar.copy(
+                out=xg[:].bitcast(F32).rearrange("q (g w u) -> q g w u", g=2, u=2),
+                in_=XT[i][:].rearrange("q (g u) w -> q g w u", g=2),
+            )
+            XG[i] = xg
+
+        def q1(i):
+            xc = ring6.tile([P, 2, P], U32, name="xc", tag="xc", align_bytes=64)
+            xs = ring6.tile([P, 2, P], U8, name="xs", tag="xs", align_bytes=64)
+            nc.vector.quantize_mx(
+                out=xc[:].rearrange("q g w -> q (g w)").bitcast(FP8X4),
+                scales=xs[:].rearrange("q g w -> q (g w)"),
+                in_=XG[i][:],
+            )
+            XC[i] = xc
+            XS[i] = xs
+
+        def m1(i):
+            a = psum.tile([P, QR], F32, name="a", tag="a")
+            for g in range(2):
+                nc.tensor.matmul_mx(
+                    out=a[:],
+                    lhsT=XC[i][:, g, :].bitcast(FP8X4),
+                    lhsT_scale=XS[i][:, g, :],
+                    rhs=wa_c[:, g, :].bitcast(FP8X4),
+                    rhs_scale=wa_s[:, g, :],
+                    start=(g == 0),
+                    stop=(g == 1),
+                )
+            A[i] = a
+
+        def cqf(i):
+            cq = ring3.tile([P, QR], BF16, name="cq", tag="cq")
+            nc.vector.scalar_tensor_tensor(
+                out=cq[:], in0=A[i][:], scalar=RA[i], in1=gam[:], op0=ALU.mult, op1=ALU.mult
+            )
+            CQ[i] = cq
+
+        def t2(i):
+            ct = psum.tile([P, 4, P], BF16, name="ct", tag="ct")
+            for t in range(4):
+                nc.tensor.transpose(ct[:, t, :], CQ[i][:, t * P : (t + 1) * P], ident_b[:])
+            CT[i] = ct
+
+        def c2(i):
+            cg = ring3.tile([P, P, 4], BF16, name="cg", tag="cg", align_bytes=64)
+            nc.scalar.copy(out=cg[:], in_=CT[i][:].rearrange("p t w -> p w t"))
+            CG[i] = cg
+
+        def q2(i):
+            cc = ring3.tile([P, P], U32, name="cc", tag="cc", align_bytes=64)
+            cs = ring3.tile([P, P], U8, name="cs", tag="cs", align_bytes=64)
+            nc.vector.quantize_mx(
+                out=cc[:].bitcast(FP8X4), scales=cs[:], in_=CG[i][:].rearrange("p w t -> p (w t)")
+            )
+            CC[i] = cc
+            CS[i] = cs
+
+        def m2(i):
+            ob = psum.tile([P, 512], F32, name="ob", tag="ob")
+            for g in range(2):
+                nc.tensor.matmul_mx(
+                    out=ob[:, 0:128],
+                    lhsT=XC[i][:, g, :].bitcast(FP8X4),
+                    lhsT_scale=XS[i][:, g, :],
+                    rhs=wk_c[:, g, :].bitcast(FP8X4),
+                    rhs_scale=wk_s[:, g, :],
+                    start=(g == 0),
+                    stop=(g == 1),
+                )
+            for (lo, hi) in ((0, 128), (128, 384)):
+                nc.tensor.matmul_mx(
+                    out=ob[:, 128 + lo : 128 + hi],
+                    lhsT=CC[i][:].bitcast(FP8X4),
+                    lhsT_scale=CS[i][:],
+                    rhs=wb_c[:, lo:hi].bitcast(FP8X4),
+                    rhs_scale=wb_s[:, lo:hi],
+                    start=True,
+                    stop=True,
+                )
+            OB[i] = ob
+
+        def stats(s):
+            ia, ik = s - 1, s - 4
+            if not (ok(ia) or ok(ik)):
+                return
+            ms = ring3.tile([P, 2], F32, name="ms", tag="ms")
+            sd = ring3.tile([P, 2], F32, name="sd", tag="sd")
+            if ok(ia):
+                nc.scalar.activation(
+                    out=junk[:],
+                    in_=A[ia][:],
+                    func=ACT.Square,
+                    scale=1.0 / math.sqrt(QR),
+                    accum_out=ms[:, 0:1],
+                )
+            if ok(ik):
+                nc.scalar.activation(
+                    out=junk[:, 0:KVR],
+                    in_=OB[ik][:, 0:KVR],
+                    func=ACT.Square,
+                    scale=1.0 / math.sqrt(KVR),
+                    accum_out=ms[:, 1:2],
+                )
+            lo = 0 if ok(ia) else 1
+            hi = 2 if ok(ik) else 1
+            nc.scalar.activation(
+                out=sd[:, lo:hi], in_=ms[:, lo:hi], func=ACT.Sqrt, bias=EPS, scale=1.0
+            )
+            ST[s] = (sd, lo, hi)
+
+        def recip(s):
+            if (s - 1) not in ST:
+                return
+            (sd, lo, hi) = ST[s - 1]
+            r2 = ring3.tile([P, 2], F32, name="r2", tag="r2")
+            nc.vector.reciprocal(out=r2[:, lo:hi], in_=sd[:, lo:hi])
+            RA[s - 2] = r2[:, 0:1]
+            RK[s - 5] = r2[:, 1:2]
+
+        def ev(i):
+            c, k = i // CH, i % CH
+            if k == 0:
+                oc = ring3.tile([P, CH, 512], F32, name="oc", tag="oc")
+                pr = ring2.tile([P, CH, 3, 2, 2, 32], F32, name="pr", tag="pr")
+                OC[c] = oc
+                PR[c] = pr
+            oc, pr, ob = OC[c], PR[c], OB[i]
+            nc.vector.scalar_tensor_tensor(
+                out=oc[:, k, 384:448],
+                in0=ob[:, 0:KVR],
+                scalar=RK[i],
+                in1=gamk[:],
+                op0=ALU.mult,
+                op1=ALU.mult,
+            )
+            nc.vector.tensor_tensor(
+                out=pr[:, k].rearrange("p g x y j -> p g x (y j)"),
+                in0=ob[:, 64:256]
+                .rearrange("p (g c) -> p g c", g=3)
+                .unsqueeze(2)
+                .to_broadcast([P, 3, 2, 64]),
+                in1=tab[:, i]
+                .rearrange("p x y j -> p x (y j)")
+                .unsqueeze(1)
+                .to_broadcast([P, 3, 2, 64]),
+                op=ALU.mult,
+            )
+            nc.vector.tensor_copy(
+                out=oc[:, k, 0:384].rearrange("p (h c) -> p h c", h=2)[:, :, 0:128],
+                in_=ob[:, 256:512].rearrange("p (h c) -> p h c", h=2),
+            )
+            if k == CH - 1:
+                nc.vector.tensor_tensor(
+                    out=oc[:, :, 0:384]
+                    .rearrange("p k (h c) -> p k h c", h=2)[:, :, :, 128:192]
+                    .rearrange("p k h (x j) -> p k h x j", x=2),
+                    in0=pr[:, :, 1:3, :, 0, :],
+                    in1=pr[:, :, 1:3, :, 1, :],
+                    op=ALU.add,
+                )
+                nc.vector.tensor_tensor(
+                    out=oc[:, :, 448:512].rearrange("p k (x j) -> p k x j", x=2),
+                    in0=pr[:, :, 0, :, 0, :],
+                    in1=pr[:, :, 0, :, 1, :],
+                    op=ALU.add,
+                )
+                nc.sync.dma_start(out=out_v[:, c * CH : (c + 1) * CH, :], in_=oc[:])
+
+        for s in range(NT + 6):
+            if ok(s):
+                t1(s)
+            if ok(s - 3):
+                t2(s - 3)
+            if s == 1:
+                prep_gamma_mm()
+            if ok(s):
+                c1(s)
+            if ok(s - 3):
+                c2(s - 3)
+            if s == 2:
+                prep_wb_copy()
+            recip(s)
+            if ok(s - 2):
+                cqf(s - 2)
+            if ok(s - 5):
+                ev(s - 5)
+            if ok(s):
+                q1(s)
+            if ok(s - 3):
+                q2(s - 3)
+            if s == 3:
+                prep_w_quant()
+            if ok(s - 1):
+                m1(s - 1)
+            if ok(s - 4):
+                m2(s - 4)
+            stats(s)

@@ -18,6 +18,9 @@ P = 128
 NT = T // P
 CH = 4
 NC = NT // CH
+OUT_GROUPS = (4, 4, 4, 4, 4, 4, 4, 2, 2)
+L_Q1, L_M1, L_CQ, L_T2, L_Q2, L_M2, L_EV = 1, 2, 4, 5, 6, 7, 8
+NOPE_ON_SCALAR_FROM = 24
 FLOPS = 2 * T * (H * (QR + KVR + DR) + QR * NH * (DN + DR))
 
 
@@ -29,8 +32,12 @@ def tile_mla_model_t_kernel(
         const = ctx.enter_context(tc.tile_pool(name="const", bufs=1))
         ring2 = ctx.enter_context(tc.tile_pool(name="ring2", bufs=2))
         ring3 = ctx.enter_context(tc.tile_pool(name="ring3", bufs=3))
-        ring6 = ctx.enter_context(tc.tile_pool(name="ring6", bufs=6))
-        psum = ctx.enter_context(tc.psum_pool(name="psum", bufs=2))
+        ring4 = ctx.enter_context(tc.tile_pool(name="ring4", bufs=4))
+        ring8 = ctx.enter_context(tc.tile_pool(name="ring8", bufs=8))
+        ps_xt = ctx.enter_context(tc.psum_pool(name="ps_xt", bufs=2))
+        ps_a = ctx.enter_context(tc.psum_pool(name="ps_a", bufs=3))
+        ps_ct = ctx.enter_context(tc.psum_pool(name="ps_ct", bufs=1))
+        ps_ob = ctx.enter_context(tc.psum_pool(name="ps_ob", bufs=2))
         ctx.enter_context(tc.manual_schedule())
 
         x_v = token_x.rearrange("(p i) h -> p i h", i=NT)
@@ -42,11 +49,6 @@ def tile_mla_model_t_kernel(
             nc.sync.dma_start(
                 out=wa_raw[:, g].rearrange("q (u e) n -> q u (e n)", u=2), in_=wa_v[:, g]
             )
-        wk_raw = const.tile([P, 2, 4, P], BF16, name="wk_raw")
-        nc.sync.dma_start(
-            out=wk_raw[:].rearrange("q g (u e) n -> q (g u) (e n)", u=2),
-            in_=wkv.rearrange("(g u q e) n -> q (g u) (e n)", g=2, u=2, q=P, e=2),
-        )
         gz = const.tile([P, QR + KVR], BF16, name="gz")
         nc.vector.memset(gz[:], 0.0)
         nc.sync.dma_start(out=gz[0:1, 0:QR], in_=gamma_cq.rearrange("(o n) -> o n", o=1))
@@ -59,6 +61,11 @@ def tile_mla_model_t_kernel(
             x_sb.append(x_c)
         nc.sync.dma_start(out=x_sb[0][:, 0:2, :], in_=x_v[:, 0:2, :])
         nc.sync.dma_start(out=x_sb[0][:, 2:4, :], in_=x_v[:, 2:4, :])
+        wk_raw = const.tile([P, 2, 4, P], BF16, name="wk_raw")
+        nc.sync.dma_start(
+            out=wk_raw[:].rearrange("q g (u e) n -> q (g u) (e n)", u=2),
+            in_=wkv.rearrange("(g u q e) n -> q (g u) (e n)", g=2, u=2, q=P, e=2),
+        )
         wb_raw = const.tile([P, 4, 384], BF16, name="wb_raw")
         nc.sync.dma_start(out=wb_raw[:], in_=wq_b.rearrange("(t p) n -> p t n", t=4))
         nc.sync.dma_start(out=x_sb[1][:], in_=x_v[:, CH : 2 * CH, :])
@@ -78,13 +85,26 @@ def tile_mla_model_t_kernel(
         warm = const.tile([P, 1], F32, name="warm")
         nc.vector.memset(warm[:], 1.0)
         warm2 = const.tile([P, 1], F32, name="warm2")
-        nc.scalar.activation(out=warm2[:], in_=warm[:], func=ACT.Sqrt)
+        nc.scalar.activation(out=warm2[:], in_=warm[:], func=ACT.Abs_reciprocal_sqrt)
         junk = const.tile([P, QR], BF16, name="junk")
         gam = const.tile([P, QR], F32, name="gam")
         gamk = const.tile([P, KVR], F32, name="gamk")
 
+        wk_g = const.tile([P, 2, P, 4], BF16, name="wk_g", align_bytes=64)
+        wb_g = const.tile([P, 384, 4], BF16, name="wb_g", align_bytes=64)
+        wb_h = wb_raw[:].rearrange("p t (h c) -> p h c t", h=2)
+        for (dst, src) in (
+            (wk_g[:], wk_raw[:].rearrange("p g t n -> p g n t")),
+            (wb_g[:, 0:128, :].rearrange("p (h c) t -> p h c t", h=2), wb_h[:, :, 128:192, :]),
+            (wb_g[:, 128:384, :].rearrange("p (h c) t -> p h c t", h=2), wb_h[:, :, 0:128, :]),
+        ):
+            nc.gpsimd.tensor_scalar(
+                out=dst, in0=src, scalar1=1.0, scalar2=0.0, op0=ALU.mult, op1=ALU.add
+            )
+
         tab = const.tile([P, NT, 2, 2, 32], BF16, name="tab")
-        for c in range(NC):
+
+        def make_tab(c):
             ii = slice(c * CH, (c + 1) * CH)
             for (xh, yh, src, lo, sign) in (
                 (0, 0, cos_sb, 0, 1.0),
@@ -101,6 +121,9 @@ def tile_mla_model_t_kernel(
                     op1=ALU.add,
                 )
 
+        make_tab(0)
+        make_tab(1)
+
         wa_g = const.tile([P, 2, QR, 4], BF16, name="wa_g", align_bytes=64)
         wa_c = const.tile([P, 2, QR], U32, name="wa_c", align_bytes=64)
         wa_s = const.tile([P, 2, QR], U8, name="wa_s", align_bytes=64)
@@ -114,24 +137,10 @@ def tile_mla_model_t_kernel(
             scales=wa_s[:].rearrange("p g n -> p (g n)"),
             in_=wa_g[:].rearrange("p g n t -> p (g n t)"),
         )
-        wk_g = const.tile([P, 2, P, 4], BF16, name="wk_g", align_bytes=64)
         wk_c = const.tile([P, 2, P], U32, name="wk_c", align_bytes=64)
         wk_s = const.tile([P, 2, P], U8, name="wk_s", align_bytes=64)
-        nc.scalar.copy(out=wk_g[:], in_=wk_raw[:].rearrange("p g t n -> p g n t"))
-        wb_g = const.tile([P, 384, 4], BF16, name="wb_g", align_bytes=64)
         wb_c = const.tile([P, 384], U32, name="wb_c", align_bytes=64)
         wb_s = const.tile([P, 384], U8, name="wb_s", align_bytes=64)
-
-        def prep_wb_copy():
-            wb_h = wb_raw[:].rearrange("p t (h c) -> p h c t", h=2)
-            nc.scalar.copy(
-                out=wb_g[:, 0:128, :].rearrange("p (h c) t -> p h c t", h=2),
-                in_=wb_h[:, :, 128:192, :],
-            )
-            nc.scalar.copy(
-                out=wb_g[:, 128:384, :].rearrange("p (h c) t -> p h c t", h=2),
-                in_=wb_h[:, :, 0:128, :],
-            )
 
         def prep_w_quant():
             nc.vector.quantize_mx(
@@ -151,9 +160,9 @@ def tile_mla_model_t_kernel(
             )
 
         def prep_gamma_mm():
-            g1 = psum.tile([P, 512], F32, name="ob", tag="ob")
+            g1 = ps_ob.tile([P, 512], F32, name="ob", tag="ob")
             nc.tensor.matmul(out=g1[:], lhsT=ones[:], rhs=gz[:, 0:QR], start=True, stop=True)
-            g2 = psum.tile([P, 512], F32, name="ob", tag="ob")
+            g2 = ps_ob.tile([P, 512], F32, name="ob", tag="ob")
             nc.tensor.matmul(
                 out=g2[:, 0:KVR], lhsT=ones[:], rhs=gz[:, QR : QR + KVR], start=True, stop=True
             )
@@ -161,13 +170,19 @@ def tile_mla_model_t_kernel(
             nc.scalar.copy(out=gamk[:], in_=g2[:, 0:KVR])
 
         XT, XG, XC, XS, A, CQ, CT, CG, CC, CS, OB = {}, {}, {}, {}, {}, {}, {}, {}, {}, {}, {}
-        ST, RA, RK, OC, PR = {}, {}, {}, {}, {}
+        MS, ST, RA, OC, PR, MK, SK = {}, {}, {}, {}, {}, {}, {}
+        GROUP = {}
+        first = 0
+        for (c, n) in enumerate(OUT_GROUPS):
+            for k in range(n):
+                GROUP[first + k] = (c, k, n)
+            first += n
 
         def ok(i):
             return 0 <= i < NT
 
         def t1(i):
-            xt = psum.tile([P, 4, P], F32, name="xt", tag="xt")
+            xt = ps_xt.tile([P, 4, P], F32, name="xt", tag="xt")
             xw = x_sb[i // CH][:, i % CH, :].bitcast(F32)
             for b in range(4):
                 nc.tensor.transpose(xt[:, b, :], xw[:, b * P : (b + 1) * P], ident_f[:])
@@ -182,8 +197,8 @@ def tile_mla_model_t_kernel(
             XG[i] = xg
 
         def q1(i):
-            xc = ring6.tile([P, 2, P], U32, name="xc", tag="xc", align_bytes=64)
-            xs = ring6.tile([P, 2, P], U8, name="xs", tag="xs", align_bytes=64)
+            xc = ring8.tile([P, 2, P], U32, name="xc", tag="xc", align_bytes=64)
+            xs = ring8.tile([P, 2, P], U8, name="xs", tag="xs", align_bytes=64)
             nc.vector.quantize_mx(
                 out=xc[:].rearrange("q g w -> q (g w)").bitcast(FP8X4),
                 scales=xs[:].rearrange("q g w -> q (g w)"),
@@ -193,7 +208,7 @@ def tile_mla_model_t_kernel(
             XS[i] = xs
 
         def m1(i):
-            a = psum.tile([P, QR], F32, name="a", tag="a")
+            a = ps_a.tile([P, QR], F32, name="a", tag="a")
             for g in range(2):
                 nc.tensor.matmul_mx(
                     out=a[:],
@@ -214,7 +229,7 @@ def tile_mla_model_t_kernel(
             CQ[i] = cq
 
         def t2(i):
-            ct = psum.tile([P, 4, P], BF16, name="ct", tag="ct")
+            ct = ps_ct.tile([P, 4, P], BF16, name="ct", tag="ct")
             for t in range(4):
                 nc.tensor.transpose(ct[:, t, :], CQ[i][:, t * P : (t + 1) * P], ident_b[:])
             CT[i] = ct
@@ -234,7 +249,7 @@ def tile_mla_model_t_kernel(
             CS[i] = cs
 
         def m2(i):
-            ob = psum.tile([P, 512], F32, name="ob", tag="ob")
+            ob = ps_ob.tile([P, 512], F32, name="ob", tag="ob")
             for g in range(2):
                 nc.tensor.matmul_mx(
                     out=ob[:, 0:128],
@@ -257,60 +272,59 @@ def tile_mla_model_t_kernel(
                 )
             OB[i] = ob
 
-        def stats(s):
-            ia, ik = s - 1, s - 4
-            if not (ok(ia) or ok(ik)):
-                return
-            ms = ring3.tile([P, 2], F32, name="ms", tag="ms")
-            sd = ring3.tile([P, 2], F32, name="sd", tag="sd")
-            if ok(ia):
-                nc.scalar.activation(
-                    out=junk[:],
-                    in_=A[ia][:],
-                    func=ACT.Square,
-                    scale=1.0 / math.sqrt(QR),
-                    accum_out=ms[:, 0:1],
-                )
-            if ok(ik):
-                nc.scalar.activation(
-                    out=junk[:, 0:KVR],
-                    in_=OB[ik][:, 0:KVR],
-                    func=ACT.Square,
-                    scale=1.0 / math.sqrt(KVR),
-                    accum_out=ms[:, 1:2],
-                )
-            lo = 0 if ok(ia) else 1
-            hi = 2 if ok(ik) else 1
+        def sq(i):
+            ms = ring4.tile([P, 1], F32, name="ms", tag="ms")
+            sd = ring4.tile([P, 1], F32, name="sd", tag="sd")
             nc.scalar.activation(
-                out=sd[:, lo:hi], in_=ms[:, lo:hi], func=ACT.Sqrt, bias=EPS, scale=1.0
+                out=junk[:],
+                in_=A[i][:],
+                func=ACT.Square,
+                scale=1.0 / math.sqrt(QR),
+                accum_out=ms[:],
             )
-            ST[s] = (sd, lo, hi)
+            MS[i] = ms
+            ST[i] = sd
 
-        def recip(s):
-            if (s - 1) not in ST:
-                return
-            (sd, lo, hi) = ST[s - 1]
-            r2 = ring3.tile([P, 2], F32, name="r2", tag="r2")
-            nc.vector.reciprocal(out=r2[:, lo:hi], in_=sd[:, lo:hi])
-            RA[s - 2] = r2[:, 0:1]
-            RK[s - 5] = r2[:, 1:2]
+        def sqrt_a(i):
+            nc.scalar.activation(
+                out=ST[i][:], in_=MS[i][:], func=ACT.Abs_reciprocal_sqrt, bias=EPS, scale=1.0
+            )
+            RA[i] = ST[i][:]
+
+        def sqk(i):
+            (c, k, n) = GROUP[i]
+            if k == 0:
+                mk = ring3.tile([P, CH], F32, name="mk", tag="mk")
+                MK[c] = mk
+            nc.scalar.activation(
+                out=junk[:, 0:KVR],
+                in_=OB[i][:, 0:KVR],
+                func=ACT.Square,
+                scale=1.0 / math.sqrt(KVR),
+                accum_out=MK[c][:, k : k + 1],
+            )
+
+        def sqrt_k(i):
+            (c, k, n) = GROUP[i]
+            if k == n - 1:
+                sk = ring3.tile([P, CH], F32, name="sk", tag="sk")
+                nc.scalar.activation(
+                    out=sk[:, 0:n],
+                    in_=MK[c][:, 0:n],
+                    func=ACT.Abs_reciprocal_sqrt,
+                    bias=EPS,
+                    scale=1.0,
+                )
+                SK[c] = sk
 
         def ev(i):
-            c, k = i // CH, i % CH
+            (c, k, n) = GROUP[i]
             if k == 0:
                 oc = ring3.tile([P, CH, 512], F32, name="oc", tag="oc")
                 pr = ring2.tile([P, CH, 3, 2, 2, 32], F32, name="pr", tag="pr")
                 OC[c] = oc
                 PR[c] = pr
             oc, pr, ob = OC[c], PR[c], OB[i]
-            nc.vector.scalar_tensor_tensor(
-                out=oc[:, k, 384:448],
-                in0=ob[:, 0:KVR],
-                scalar=RK[i],
-                in1=gamk[:],
-                op0=ALU.mult,
-                op1=ALU.mult,
-            )
             nc.vector.tensor_tensor(
                 out=pr[:, k].rearrange("p g x y j -> p g x (y j)"),
                 in0=ob[:, 64:256]
@@ -323,53 +337,80 @@ def tile_mla_model_t_kernel(
                 .to_broadcast([P, 3, 2, 64]),
                 op=ALU.mult,
             )
-            nc.vector.tensor_copy(
-                out=oc[:, k, 0:384].rearrange("p (h c) -> p h c", h=2)[:, :, 0:128],
-                in_=ob[:, 256:512].rearrange("p (h c) -> p h c", h=2),
+            nc.vector.tensor_tensor(
+                out=oc[:, k, 384:448], in0=ob[:, 0:KVR], in1=gamk[:], op=ALU.mult
             )
-            if k == CH - 1:
-                nc.vector.tensor_tensor(
-                    out=oc[:, :, 0:384]
-                    .rearrange("p k (h c) -> p k h c", h=2)[:, :, :, 128:192]
-                    .rearrange("p k h (x j) -> p k h x j", x=2),
-                    in0=pr[:, :, 1:3, :, 0, :],
-                    in1=pr[:, :, 1:3, :, 1, :],
-                    op=ALU.add,
-                )
-                nc.vector.tensor_tensor(
-                    out=oc[:, :, 448:512].rearrange("p k (x j) -> p k x j", x=2),
-                    in0=pr[:, :, 0, :, 0, :],
-                    in1=pr[:, :, 0, :, 1, :],
-                    op=ALU.add,
-                )
-                nc.sync.dma_start(out=out_v[:, c * CH : (c + 1) * CH, :], in_=oc[:])
+            nc.gpsimd.tensor_tensor(
+                out=oc[:, k, 0:384]
+                .rearrange("p (h c) -> p h c", h=2)[:, :, 128:192]
+                .rearrange("p h (x j) -> p h x j", x=2),
+                in0=pr[:, k, 1:3, :, 0, :],
+                in1=pr[:, k, 1:3, :, 1, :],
+                op=ALU.add,
+            )
+            nc.gpsimd.tensor_tensor(
+                out=oc[:, k, 448:512].rearrange("p (x j) -> p x j", x=2),
+                in0=pr[:, k, 0, :, 0, :],
+                in1=pr[:, k, 0, :, 1, :],
+                op=ALU.add,
+            )
 
-        for s in range(NT + 6):
+        def ev_nope(i):
+            (c, k, n) = GROUP[i]
+            dst = OC[c][:, k, 0:384].rearrange("p (h c) -> p h c", h=2)[:, :, 0:128]
+            src = OB[i][:, 256:512].rearrange("p (h c) -> p h c", h=2)
+            if i >= NOPE_ON_SCALAR_FROM:
+                nc.scalar.copy(out=dst, in_=src)
+            else:
+                nc.vector.tensor_copy(out=dst, in_=src)
+
+        def ev_fin(i):
+            (c, k, n) = GROUP[i]
+            oc = OC[c]
+            if k == n - 1:
+                nc.vector.tensor_tensor(
+                    out=oc[:, 0:n, 384:448],
+                    in0=oc[:, 0:n, 384:448],
+                    in1=SK[c][:, 0:n].unsqueeze(2).to_broadcast([P, n, KVR]),
+                    op=ALU.mult,
+                )
+                nc.sync.dma_start(out=out_v[:, i - n + 1 : i + 1, :], in_=oc[:, 0:n, :])
+
+        for s in range(NT + L_EV + 1):
             if ok(s):
                 t1(s)
-            if ok(s - 3):
-                t2(s - 3)
+            if ok(s - L_T2):
+                t2(s - L_T2)
             if s == 1:
                 prep_gamma_mm()
             if ok(s):
                 c1(s)
-            if ok(s - 3):
-                c2(s - 3)
-            if s == 2:
-                prep_wb_copy()
-            recip(s)
-            if ok(s - 2):
-                cqf(s - 2)
-            if ok(s - 5):
-                ev(s - 5)
-            if ok(s):
-                q1(s)
-            if ok(s - 3):
-                q2(s - 3)
-            if s == 3:
+            if ok(s - L_T2):
+                c2(s - L_T2)
+            if ok(s - L_Q1):
+                q1(s - L_Q1)
+            if ok(s - L_Q2):
+                q2(s - L_Q2)
+            if s % CH == 0 and 2 <= s // CH + 1 < NC:
+                make_tab(s // CH + 1)
+            if ok(s - L_EV):
+                ev(s - L_EV)
+            if ok(s - L_CQ):
+                cqf(s - L_CQ)
+            if ok(s - L_EV):
+                ev_nope(s - L_EV)
+                ev_fin(s - L_EV)
+            if s == 5:
                 prep_w_quant()
-            if ok(s - 1):
-                m1(s - 1)
-            if ok(s - 4):
-                m2(s - 4)
-            stats(s)
+            if ok(s - L_M1):
+                m1(s - L_M1)
+            if ok(s - L_M2):
+                m2(s - L_M2)
+            if ok(s - L_M1):
+                sq(s - L_M1)
+            if ok(s - L_M2):
+                sqk(s - L_M2)
+            if ok(s - L_M1):
+                sqrt_a(s - L_M1)
+            if ok(s - L_M2):
+                sqrt_k(s - L_M2)

@@ -34,9 +34,8 @@ def tile_mla_model_t_kernel(
         ring3 = ctx.enter_context(tc.tile_pool(name="ring3", bufs=3))
         ring4 = ctx.enter_context(tc.tile_pool(name="ring4", bufs=4))
         ring8 = ctx.enter_context(tc.tile_pool(name="ring8", bufs=8))
-        ps_xt = ctx.enter_context(tc.psum_pool(name="ps_xt", bufs=2))
+        ps_tp = ctx.enter_context(tc.psum_pool(name="ps_tp", bufs=3))
         ps_a = ctx.enter_context(tc.psum_pool(name="ps_a", bufs=3))
-        ps_ct = ctx.enter_context(tc.psum_pool(name="ps_ct", bufs=1))
         ps_ob = ctx.enter_context(tc.psum_pool(name="ps_ob", bufs=2))
         ctx.enter_context(tc.manual_schedule())
 
@@ -93,36 +92,32 @@ def tile_mla_model_t_kernel(
         wk_g = const.tile([P, 2, P, 4], BF16, name="wk_g", align_bytes=64)
         wb_g = const.tile([P, 384, 4], BF16, name="wb_g", align_bytes=64)
         wb_h = wb_raw[:].rearrange("p t (h c) -> p h c t", h=2)
-        for (dst, src) in (
-            (wk_g[:], wk_raw[:].rearrange("p g t n -> p g n t")),
-            (wb_g[:, 0:128, :].rearrange("p (h c) t -> p h c t", h=2), wb_h[:, :, 128:192, :]),
-            (wb_g[:, 128:384, :].rearrange("p (h c) t -> p h c t", h=2), wb_h[:, :, 0:128, :]),
-        ):
-            nc.gpsimd.tensor_scalar(
-                out=dst, in0=src, scalar1=1.0, scalar2=0.0, op0=ALU.mult, op1=ALU.add
-            )
+
+        def prep_w_regroup():
+            for (dst, src) in (
+                (wk_g[:], wk_raw[:].rearrange("p g t n -> p g n t")),
+                (wb_g[:, 0:128, :].rearrange("p (h c) t -> p h c t", h=2), wb_h[:, :, 128:192, :]),
+                (wb_g[:, 128:384, :].rearrange("p (h c) t -> p h c t", h=2), wb_h[:, :, 0:128, :]),
+            ):
+                nc.vector.tensor_copy(out=dst, in_=src)
 
         tab = const.tile([P, NT, 2, 2, 32], BF16, name="tab")
 
-        def make_tab(c):
-            ii = slice(c * CH, (c + 1) * CH)
+        def make_tab():
             for (xh, yh, src, lo, sign) in (
                 (0, 0, cos_sb, 0, 1.0),
                 (0, 1, sin_sb, 0, -1.0),
                 (1, 0, sin_sb, 32, 1.0),
                 (1, 1, cos_sb, 32, 1.0),
             ):
-                nc.gpsimd.tensor_scalar(
-                    out=tab[:, ii, xh, yh, :],
-                    in0=src[:, ii, lo : lo + 32],
+                nc.vector.tensor_scalar(
+                    out=tab[:, :, xh, yh, :],
+                    in0=src[:, :, lo : lo + 32],
                     scalar1=sign,
                     scalar2=0.0,
                     op0=ALU.mult,
                     op1=ALU.add,
                 )
-
-        make_tab(0)
-        make_tab(1)
 
         wa_g = const.tile([P, 2, QR, 4], BF16, name="wa_g", align_bytes=64)
         wa_c = const.tile([P, 2, QR], U32, name="wa_c", align_bytes=64)
@@ -182,7 +177,7 @@ def tile_mla_model_t_kernel(
             return 0 <= i < NT
 
         def t1(i):
-            xt = ps_xt.tile([P, 4, P], F32, name="xt", tag="xt")
+            xt = ps_tp.tile([P, 4, P], F32, name="xt", tag="tp")
             xw = x_sb[i // CH][:, i % CH, :].bitcast(F32)
             for b in range(4):
                 nc.tensor.transpose(xt[:, b, :], xw[:, b * P : (b + 1) * P], ident_f[:])
@@ -229,7 +224,7 @@ def tile_mla_model_t_kernel(
             CQ[i] = cq
 
         def t2(i):
-            ct = ps_ct.tile([P, 4, P], BF16, name="ct", tag="ct")
+            ct = ps_tp.tile([P, 4, P], BF16, name="ct", tag="tp")
             for t in range(4):
                 nc.tensor.transpose(ct[:, t, :], CQ[i][:, t * P : (t + 1) * P], ident_b[:])
             CT[i] = ct
@@ -385,14 +380,16 @@ def tile_mla_model_t_kernel(
                 prep_gamma_mm()
             if ok(s):
                 c1(s)
+            if ok(s - L_M1 - 1):
+                sqrt_a(s - L_M1 - 1)
+            if ok(s - L_M2 - 1):
+                sqrt_k(s - L_M2 - 1)
             if ok(s - L_T2):
                 c2(s - L_T2)
             if ok(s - L_Q1):
                 q1(s - L_Q1)
             if ok(s - L_Q2):
                 q2(s - L_Q2)
-            if s % CH == 0 and 2 <= s // CH + 1 < NC:
-                make_tab(s // CH + 1)
             if ok(s - L_EV):
                 ev(s - L_EV)
             if ok(s - L_CQ):
@@ -400,8 +397,12 @@ def tile_mla_model_t_kernel(
             if ok(s - L_EV):
                 ev_nope(s - L_EV)
                 ev_fin(s - L_EV)
-            if s == 5:
+            if s == 3:
+                prep_w_regroup()
+            if s == 4:
                 prep_w_quant()
+            if s == 6:
+                make_tab()
             if ok(s - L_M1):
                 m1(s - L_M1)
             if ok(s - L_M2):
@@ -410,7 +411,3 @@ def tile_mla_model_t_kernel(
                 sq(s - L_M1)
             if ok(s - L_M2):
                 sqk(s - L_M2)
-            if ok(s - L_M1):
-                sqrt_a(s - L_M1)
-            if ok(s - L_M2):
-                sqrt_k(s - L_M2)

@@ -66,7 +66,10 @@ def tile_mla_model_t_kernel(
             in_=wkv.rearrange("(g u q e) n -> q (g u) (e n)", g=2, u=2, q=P, e=2),
         )
         wb_raw = const.tile([P, 4, 384], BF16, name="wb_raw")
-        nc.sync.dma_start(out=wb_raw[:], in_=wq_b.rearrange("(t p) n -> p t n", t=4))
+        nc.sync.dma_start(
+            out=wb_raw[:].rearrange("q (u e) n -> q u (e n)", u=2),
+            in_=wq_b.rearrange("(u q e) n -> q u (e n)", u=2, q=P, e=2),
+        )
         nc.sync.dma_start(out=x_sb[1][:], in_=x_v[:, CH : 2 * CH, :])
         cos_sb = const.tile([P, NT, DR], BF16, name="cos_sb")
         sin_sb = const.tile([P, NT, DR], BF16, name="sin_sb")
@@ -77,8 +80,6 @@ def tile_mla_model_t_kernel(
 
         ident_f = const.tile([P, P], F32, name="ident_f")
         make_identity(nc, ident_f[:])
-        ident_b = const.tile([P, P], BF16, name="ident_b")
-        make_identity(nc, ident_b[:])
         ones = const.tile([P, P], BF16, name="ones")
         nc.vector.memset(ones[:], 1.0)
         warm = const.tile([P, 1], F32, name="warm")
@@ -224,14 +225,18 @@ def tile_mla_model_t_kernel(
             CQ[i] = cq
 
         def t2(i):
-            ct = ps_tp.tile([P, 4, P], BF16, name="ct", tag="tp")
-            for t in range(4):
-                nc.tensor.transpose(ct[:, t, :], CQ[i][:, t * P : (t + 1) * P], ident_b[:])
+            ct = ps_tp.tile([P, 2, P], F32, name="ct", tag="tp")
+            cw = CQ[i][:].bitcast(F32)
+            for u in range(2):
+                nc.tensor.transpose(ct[:, u, :], cw[:, u * P : (u + 1) * P], ident_f[:])
             CT[i] = ct
 
         def c2(i):
             cg = ring3.tile([P, P, 4], BF16, name="cg", tag="cg", align_bytes=64)
-            nc.scalar.copy(out=cg[:], in_=CT[i][:].rearrange("p t w -> p w t"))
+            nc.scalar.copy(
+                out=cg[:].rearrange("p w t -> p (w t)").bitcast(F32).rearrange("p (w u) -> p w u", u=2),
+                in_=CT[i][:].rearrange("p u w -> p w u"),
+            )
             CG[i] = cg
 
         def q2(i):

@@ -317,14 +317,21 @@ def tile_mla_model_t_kernel(
                 )
                 SK[c] = sk
 
+        def nope_on_scalar(i):
+            return i >= NOPE_ON_SCALAR_FROM or i % 2 == 1
+
+        def get_oc(c):
+            if c not in OC:
+                oc = ring3.tile([P, CH, 512], F32, name="oc", tag="oc")
+                OC[c] = oc
+            return OC[c]
+
         def ev(i):
             (c, k, n) = GROUP[i]
             if k == 0:
-                oc = ring3.tile([P, CH, 512], F32, name="oc", tag="oc")
                 pr = ring2.tile([P, CH, 3, 2, 2, 32], F32, name="pr", tag="pr")
-                OC[c] = oc
                 PR[c] = pr
-            oc, pr, ob = OC[c], PR[c], OB[i]
+            oc, pr, ob = get_oc(c), PR[c], OB[i]
             nc.vector.tensor_tensor(
                 out=pr[:, k].rearrange("p g x y j -> p g x (y j)"),
                 in0=ob[:, 64:256]
@@ -355,11 +362,13 @@ def tile_mla_model_t_kernel(
                 op=ALU.add,
             )
 
-        def ev_nope(i):
+        def ev_nope(i, on_scalar):
+            if nope_on_scalar(i) != on_scalar:
+                return
             (c, k, n) = GROUP[i]
-            dst = OC[c][:, k, 0:384].rearrange("p (h c) -> p h c", h=2)[:, :, 0:128]
+            dst = get_oc(c)[:, k, 0:384].rearrange("p (h c) -> p h c", h=2)[:, :, 0:128]
             src = OB[i][:, 256:512].rearrange("p (h c) -> p h c", h=2)
-            if i >= NOPE_ON_SCALAR_FROM:
+            if on_scalar:
                 nc.scalar.copy(out=dst, in_=src)
             else:
                 nc.vector.tensor_copy(out=dst, in_=src)
@@ -383,6 +392,8 @@ def tile_mla_model_t_kernel(
                 t2(s - L_T2)
             if s == 1:
                 prep_gamma_mm()
+            if ok(s - L_EV):
+                ev_nope(s - L_EV, True)
             if ok(s):
                 c1(s)
             if ok(s - L_M1 - 1):
@@ -391,16 +402,16 @@ def tile_mla_model_t_kernel(
                 sqrt_k(s - L_M2 - 1)
             if ok(s - L_T2):
                 c2(s - L_T2)
+            if ok(s - L_CQ):
+                cqf(s - L_CQ)
             if ok(s - L_Q1):
                 q1(s - L_Q1)
             if ok(s - L_Q2):
                 q2(s - L_Q2)
             if ok(s - L_EV):
                 ev(s - L_EV)
-            if ok(s - L_CQ):
-                cqf(s - L_CQ)
             if ok(s - L_EV):
-                ev_nope(s - L_EV)
+                ev_nope(s - L_EV, False)
                 ev_fin(s - L_EV)
             if s == 3:
                 prep_w_regroup()

@@ -59,7 +59,6 @@ def tile_mla_model_t_kernel(
             x_c = const.tile([P, CH, H], BF16, name="x%d" % c)
             x_sb.append(x_c)
         nc.sync.dma_start(out=x_sb[0][:, 0:2, :], in_=x_v[:, 0:2, :])
-        nc.sync.dma_start(out=x_sb[0][:, 2:4, :], in_=x_v[:, 2:4, :])
         wk_raw = const.tile([P, 2, 4, P], BF16, name="wk_raw")
         nc.sync.dma_start(
             out=wk_raw[:].rearrange("q g (u e) n -> q (g u) (e n)", u=2),
@@ -70,6 +69,7 @@ def tile_mla_model_t_kernel(
             out=wb_raw[:].rearrange("q (u e) n -> q u (e n)", u=2),
             in_=wq_b.rearrange("(u q e) n -> q u (e n)", u=2, q=P, e=2),
         )
+        nc.sync.dma_start(out=x_sb[0][:, 2:4, :], in_=x_v[:, 2:4, :])
         nc.sync.dma_start(out=x_sb[1][:], in_=x_v[:, CH : 2 * CH, :])
         cos_sb = const.tile([P, NT, DR], BF16, name="cos_sb")
         sin_sb = const.tile([P, NT, DR], BF16, name="sin_sb")
@@ -94,13 +94,13 @@ def tile_mla_model_t_kernel(
         wb_g = const.tile([P, 384, 4], BF16, name="wb_g", align_bytes=64)
         wb_h = wb_raw[:].rearrange("p t (h c) -> p h c t", h=2)
 
-        def prep_w_regroup():
-            for (dst, src) in (
+        def prep_w_regroup(which):
+            (dst, src) = (
                 (wk_g[:], wk_raw[:].rearrange("p g t n -> p g n t")),
                 (wb_g[:, 0:128, :].rearrange("p (h c) t -> p h c t", h=2), wb_h[:, :, 128:192, :]),
                 (wb_g[:, 128:384, :].rearrange("p (h c) t -> p h c t", h=2), wb_h[:, :, 0:128, :]),
-            ):
-                nc.vector.tensor_copy(out=dst, in_=src)
+            )[which]
+            nc.vector.tensor_copy(out=dst, in_=src)
 
         tab = const.tile([P, NT, 2, 2, 32], BF16, name="tab")
 
@@ -249,7 +249,10 @@ def tile_mla_model_t_kernel(
             CS[i] = cs
 
         def m2(i):
-            ob = ps_ob.tile([P, 512], F32, name="ob", tag="ob")
+            if i < NT - 3:
+                ob = ps_ob.tile([P, 512], F32, name="ob", tag="ob")
+            else:
+                ob = ps_a.tile([P, 512], F32, name="a", tag="a")
             for g in range(2):
                 nc.tensor.matmul_mx(
                     out=ob[:, 0:128],
@@ -347,7 +350,8 @@ def tile_mla_model_t_kernel(
             nc.vector.tensor_tensor(
                 out=oc[:, k, 384:448], in0=ob[:, 0:KVR], in1=gamk[:], op=ALU.mult
             )
-            nc.gpsimd.tensor_tensor(
+            add_eng = nc.vector if i == NT - 1 else nc.gpsimd
+            add_eng.tensor_tensor(
                 out=oc[:, k, 0:384]
                 .rearrange("p (h c) -> p h c", h=2)[:, :, 128:192]
                 .rearrange("p h (x j) -> p h x j", x=2),
@@ -355,7 +359,7 @@ def tile_mla_model_t_kernel(
                 in1=pr[:, k, 1:3, :, 1, :],
                 op=ALU.add,
             )
-            nc.gpsimd.tensor_tensor(
+            add_eng.tensor_tensor(
                 out=oc[:, k, 448:512].rearrange("p (x j) -> p x j", x=2),
                 in0=pr[:, k, 0, :, 0, :],
                 in1=pr[:, k, 0, :, 1, :],
@@ -377,7 +381,8 @@ def tile_mla_model_t_kernel(
             (c, k, n) = GROUP[i]
             oc = OC[c]
             if k == n - 1:
-                nc.vector.tensor_tensor(
+                fin_eng = nc.vector if i == NT - 1 else nc.gpsimd
+                fin_eng.tensor_tensor(
                     out=oc[:, 0:n, 384:448],
                     in0=oc[:, 0:n, 384:448],
                     in1=SK[c][:, 0:n].unsqueeze(2).to_broadcast([P, n, KVR]),
@@ -413,9 +418,9 @@ def tile_mla_model_t_kernel(
             if ok(s - L_EV):
                 ev_nope(s - L_EV, False)
                 ev_fin(s - L_EV)
+            if s < 3:
+                prep_w_regroup(s)
             if s == 3:
-                prep_w_regroup()
-            if s == 4:
                 prep_w_quant()
             if s == 6:
                 make_tab()

@@ -321,7 +321,7 @@ def tile_mla_model_t_kernel(
                 SK[c] = sk
 
         def nope_on_scalar(i):
-            return i >= NOPE_ON_SCALAR_FROM or i % 2 == 1
+            return i >= NOPE_ON_SCALAR_FROM or i % 4 == 1
 
         def get_oc(c):
             if c not in OC:

from contextlib import ExitStack
import math

import concourse.mybir as mybir
from concourse.masks import make_identity

F32 = mybir.dt.float32
BF16 = mybir.dt.bfloat16
U32 = mybir.dt.uint32
U8 = mybir.dt.uint8
FP8X4 = mybir.dt.float8_e4m3fn_x4
ACT = mybir.ActivationFunctionType
ALU = mybir.AluOpType

T, H, QR, NH, DN, DR, KVR = 4096, 1024, 512, 2, 128, 64, 64
EPS = 1e-6
P = 128
NT = T // P
CH = 4
NC = NT // CH
OUT_GROUPS = (4, 4, 4, 4, 4, 4, 4, 2, 2)
L_Q1, L_M1, L_CQ, L_T2, L_Q2, L_M2, L_EV = 1, 2, 4, 5, 6, 7, 8
NOPE_ON_SCALAR_FROM = 24
FLOPS = 2 * T * (H * (QR + KVR + DR) + QR * NH * (DN + DR))


def tile_mla_model_t_kernel(
    tc, token_x, wq_a, wq_b, wkv, rope_cos, rope_sin, gamma_cq, gamma_ckv, out
):
    nc = tc.nc
    with ExitStack() as ctx:
        const = ctx.enter_context(tc.tile_pool(name="const", bufs=1))
        ring2 = ctx.enter_context(tc.tile_pool(name="ring2", bufs=2))
        ring3 = ctx.enter_context(tc.tile_pool(name="ring3", bufs=3))
        ring4 = ctx.enter_context(tc.tile_pool(name="ring4", bufs=4))
        ring8 = ctx.enter_context(tc.tile_pool(name="ring8", bufs=8))
        ps_tp = ctx.enter_context(tc.psum_pool(name="ps_tp", bufs=3))
        ps_a = ctx.enter_context(tc.psum_pool(name="ps_a", bufs=3))
        ps_ob = ctx.enter_context(tc.psum_pool(name="ps_ob", bufs=2))
        ctx.enter_context(tc.manual_schedule())

        x_v = token_x.rearrange("(p i) h -> p i h", i=NT)
        out_v = out.rearrange("(p i) c -> p i c", i=NT)

        wa_raw = const.tile([P, 2, 4, QR], BF16, name="wa_raw")
        wa_v = wq_a.rearrange("(g u q e) n -> q g u (e n)", g=2, u=2, q=P, e=2)
        for g in range(2):
            nc.sync.dma_start(
                out=wa_raw[:, g].rearrange("q (u e) n -> q u (e n)", u=2), in_=wa_v[:, g]
            )
        gz = const.tile([P, QR + KVR], BF16, name="gz")
        nc.vector.memset(gz[:], 0.0)
        nc.sync.dma_start(out=gz[0:1, 0:QR], in_=gamma_cq.rearrange("(o n) -> o n", o=1))
        nc.sync.dma_start(
            out=gz[0:1, QR : QR + KVR], in_=gamma_ckv.rearrange("(o n) -> o n", o=1)
        )
        x_sb = []
        for c in range(NC):
            x_c = const.tile([P, CH, H], BF16, name="x%d" % c)
            x_sb.append(x_c)
        nc.sync.dma_start(out=x_sb[0][:, 0:2, :], in_=x_v[:, 0:2, :])
        wk_raw = const.tile([P, 2, 4, P], BF16, name="wk_raw")
        nc.sync.dma_start(
            out=wk_raw[:].rearrange("q g (u e) n -> q (g u) (e n)", u=2),
            in_=wkv.rearrange("(g u q e) n -> q (g u) (e n)", g=2, u=2, q=P, e=2),
        )
        wb_raw = const.tile([P, 4, 384], BF16, name="wb_raw")
        nc.sync.dma_start(
            out=wb_raw[:].rearrange("q (u e) n -> q u (e n)", u=2),
            in_=wq_b.rearrange("(u q e) n -> q u (e n)", u=2, q=P, e=2),
        )
        nc.sync.dma_start(out=x_sb[0][:, 2:4, :], in_=x_v[:, 2:4, :])
        nc.sync.dma_start(out=x_sb[1][:], in_=x_v[:, CH : 2 * CH, :])
        cos_sb = const.tile([P, NT, DR], BF16, name="cos_sb")
        sin_sb = const.tile([P, NT, DR], BF16, name="sin_sb")
        nc.sync.dma_start(out=cos_sb[:], in_=rope_cos.rearrange("(p i) d -> p i d", i=NT))
        nc.sync.dma_start(out=sin_sb[:], in_=rope_sin.rearrange("(p i) d -> p i d", i=NT))
        for c in range(2, NC):
            nc.sync.dma_start(out=x_sb[c][:], in_=x_v[:, c * CH : (c + 1) * CH, :])

        ident_f = const.tile([P, P], F32, name="ident_f")
        make_identity(nc, ident_f[:])
        ones = const.tile([P, P], BF16, name="ones")
        nc.vector.memset(ones[:], 1.0)
        warm = const.tile([P, 1], F32, name="warm")
        nc.vector.memset(warm[:], 1.0)
        warm2 = const.tile([P, 1], F32, name="warm2")
        nc.scalar.activation(out=warm2[:], in_=warm[:], func=ACT.Abs_reciprocal_sqrt)
        junk = const.tile([P, QR], BF16, name="junk")
        gam = const.tile([P, QR], F32, name="gam")
        gamk = const.tile([P, KVR], F32, name="gamk")

        wk_g = const.tile([P, 2, P, 4], BF16, name="wk_g", align_bytes=64)
        wb_g = const.tile([P, 384, 4], BF16, name="wb_g", align_bytes=64)
        wb_h = wb_raw[:].rearrange("p t (h c) -> p h c t", h=2)

        def prep_w_regroup(which):
            (dst, src) = (
                (wk_g[:], wk_raw[:].rearrange("p g t n -> p g n t")),
                (wb_g[:, 0:128, :].rearrange("p (h c) t -> p h c t", h=2), wb_h[:, :, 128:192, :]),
                (wb_g[:, 128:384, :].rearrange("p (h c) t -> p h c t", h=2), wb_h[:, :, 0:128, :]),
            )[which]
            nc.vector.tensor_copy(out=dst, in_=src)

        tab = const.tile([P, NT, 2, 2, 32], BF16, name="tab")

        def make_tab():
            for (xh, yh, src, lo, sign) in (
                (0, 0, cos_sb, 0, 1.0),
                (0, 1, sin_sb, 0, -1.0),
                (1, 0, sin_sb, 32, 1.0),
                (1, 1, cos_sb, 32, 1.0),
            ):
                nc.vector.tensor_scalar(
                    out=tab[:, :, xh, yh, :],
                    in0=src[:, :, lo : lo + 32],
                    scalar1=sign,
                    scalar2=0.0,
                    op0=ALU.mult,
                    op1=ALU.add,
                )

        wa_g = const.tile([P, 2, QR, 4], BF16, name="wa_g", align_bytes=64)
        wa_c = const.tile([P, 2, QR], U32, name="wa_c", align_bytes=64)
        wa_s = const.tile([P, 2, QR], U8, name="wa_s", align_bytes=64)
        for g in range(2):
            nc.vector.tensor_copy(
                out=wa_g[:, g].rearrange("p (c i) t -> p c t i", i=4),
                in_=wa_raw[:, g].rearrange("p t (c i) -> p c t i", i=4),
            )
        nc.vector.quantize_mx(
            out=wa_c[:].rearrange("p g n -> p (g n)").bitcast(FP8X4),
            scales=wa_s[:].rearrange("p g n -> p (g n)"),
            in_=wa_g[:].rearrange("p g n t -> p (g n t)"),
        )
        wk_c = const.tile([P, 2, P], U32, name="wk_c", align_bytes=64)
        wk_s = const.tile([P, 2, P], U8, name="wk_s", align_bytes=64)
        wb_c = const.tile([P, 384], U32, name="wb_c", align_bytes=64)
        wb_s = const.tile([P, 384], U8, name="wb_s", align_bytes=64)

        def prep_w_quant():
            nc.vector.quantize_mx(
                out=wk_c[:].rearrange("p g n -> p (g n)").bitcast(FP8X4),
                scales=wk_s[:].rearrange("p g n -> p (g n)"),
                in_=wk_g[:].rearrange("p g n t -> p (g n t)"),
            )
            nc.vector.quantize_mx(
                out=wb_c[:, 0:128].bitcast(FP8X4),
                scales=wb_s[:, 0:128],
                in_=wb_g[:, 0:128, :].rearrange("p n t -> p (n t)"),
            )
            nc.vector.quantize_mx(
                out=wb_c[:, 128:384].bitcast(FP8X4),
                scales=wb_s[:, 128:384],
                in_=wb_g[:, 128:384, :].rearrange("p n t -> p (n t)"),
            )

        def prep_gamma_mm():
            g1 = ps_ob.tile([P, 512], F32, name="ob", tag="ob")
            nc.tensor.matmul(out=g1[:], lhsT=ones[:], rhs=gz[:, 0:QR], start=True, stop=True)
            g2 = ps_ob.tile([P, 512], F32, name="ob", tag="ob")
            nc.tensor.matmul(
                out=g2[:, 0:KVR], lhsT=ones[:], rhs=gz[:, QR : QR + KVR], start=True, stop=True
            )
            nc.scalar.copy(out=gam[:], in_=g1[:])
            nc.scalar.copy(out=gamk[:], in_=g2[:, 0:KVR])

        XT, XG, XC, XS, A, CQ, CT, CG, CC, CS, OB = {}, {}, {}, {}, {}, {}, {}, {}, {}, {}, {}
        MS, ST, RA, OC, PR, MK, SK = {}, {}, {}, {}, {}, {}, {}
        GROUP = {}
        first = 0
        for (c, n) in enumerate(OUT_GROUPS):
            for k in range(n):
                GROUP[first + k] = (c, k, n)
            first += n

        def ok(i):
            return 0 <= i < NT

        def t1(i):
            xt = ps_tp.tile([P, 4, P], F32, name="xt", tag="tp")
            xw = x_sb[i // CH][:, i % CH, :].bitcast(F32)
            for b in range(4):
                nc.tensor.transpose(xt[:, b, :], xw[:, b * P : (b + 1) * P], ident_f[:])
            XT[i] = xt

        def c1(i):
            xg = ring3.tile([P, 2 * P * 4], BF16, name="xg", tag="xg", align_bytes=64)
            nc.scalar.copy(
                out=xg[:].bitcast(F32).rearrange("q (g w u) -> q g w u", g=2, u=2),
                in_=XT[i][:].rearrange("q (g u) w -> q g w u", g=2),
            )
            XG[i] = xg

        def q1(i):
            xc = ring8.tile([P, 2, P], U32, name="xc", tag="xc", align_bytes=64)
            xs = ring8.tile([P, 2, P], U8, name="xs", tag="xs", align_bytes=64)
            nc.vector.quantize_mx(
                out=xc[:].rearrange("q g w -> q (g w)").bitcast(FP8X4),
                scales=xs[:].rearrange("q g w -> q (g w)"),
                in_=XG[i][:],
            )
            XC[i] = xc
            XS[i] = xs

        def m1(i):
            a = ps_a.tile([P, QR], F32, name="a", tag="a")
            for g in range(2):
                nc.tensor.matmul_mx(
                    out=a[:],
                    lhsT=XC[i][:, g, :].bitcast(FP8X4),
                    lhsT_scale=XS[i][:, g, :],
                    rhs=wa_c[:, g, :].bitcast(FP8X4),
                    rhs_scale=wa_s[:, g, :],
                    start=(g == 0),
                    stop=(g == 1),
                )
            A[i] = a

        def cqf(i):
            cq = ring3.tile([P, QR], BF16, name="cq", tag="cq")
            nc.vector.scalar_tensor_tensor(
                out=cq[:], in0=A[i][:], scalar=RA[i], in1=gam[:], op0=ALU.mult, op1=ALU.mult
            )
            CQ[i] = cq

        def t2(i):
            ct = ps_tp.tile([P, 2, P], F32, name="ct", tag="tp")
            cw = CQ[i][:].bitcast(F32)
            for u in range(2):
                nc.tensor.transpose(ct[:, u, :], cw[:, u * P : (u + 1) * P], ident_f[:])
            CT[i] = ct

        def c2(i):
            cg = ring3.tile([P, P, 4], BF16, name="cg", tag="cg", align_bytes=64)
            nc.scalar.copy(
                out=cg[:].rearrange("p w t -> p (w t)").bitcast(F32).rearrange("p (w u) -> p w u", u=2),
                in_=CT[i][:].rearrange("p u w -> p w u"),
            )
            CG[i] = cg

        def q2(i):
            cc = ring3.tile([P, P], U32, name="cc", tag="cc", align_bytes=64)
            cs = ring3.tile([P, P], U8, name="cs", tag="cs", align_bytes=64)
            nc.vector.quantize_mx(
                out=cc[:].bitcast(FP8X4), scales=cs[:], in_=CG[i][:].rearrange("p w t -> p (w t)")
            )
            CC[i] = cc
            CS[i] = cs

        def m2(i):
            if i < NT - 3:
                ob = ps_ob.tile([P, 512], F32, name="ob", tag="ob")
            else:
                ob = ps_a.tile([P, 512], F32, name="a", tag="a")
            for g in range(2):
                nc.tensor.matmul_mx(
                    out=ob[:, 0:128],
                    lhsT=XC[i][:, g, :].bitcast(FP8X4),
                    lhsT_scale=XS[i][:, g, :],
                    rhs=wk_c[:, g, :].bitcast(FP8X4),
                    rhs_scale=wk_s[:, g, :],
                    start=(g == 0),
                    stop=(g == 1),
                )
            for (lo, hi) in ((0, 128), (128, 384)):
                nc.tensor.matmul_mx(
                    out=ob[:, 128 + lo : 128 + hi],
                    lhsT=CC[i][:].bitcast(FP8X4),
                    lhsT_scale=CS[i][:],
                    rhs=wb_c[:, lo:hi].bitcast(FP8X4),
                    rhs_scale=wb_s[:, lo:hi],
                    start=True,
                    stop=True,
                )
            OB[i] = ob

        def sq(i):
            ms = ring4.tile([P, 1], F32, name="ms", tag="ms")
            sd = ring4.tile([P, 1], F32, name="sd", tag="sd")
            nc.scalar.activation(
                out=junk[:],
                in_=A[i][:],
                func=ACT.Square,
                scale=1.0 / math.sqrt(QR),
                accum_out=ms[:],
            )
            MS[i] = ms
            ST[i] = sd

        def sqrt_a(i):
            nc.scalar.activation(
                out=ST[i][:], in_=MS[i][:], func=ACT.Abs_reciprocal_sqrt, bias=EPS, scale=1.0
            )
            RA[i] = ST[i][:]

        def sqk(i):
            (c, k, n) = GROUP[i]
            if k == 0:
                mk = ring3.tile([P, CH], F32, name="mk", tag="mk")
                MK[c] = mk
            nc.scalar.activation(
                out=junk[:, 0:KVR],
                in_=OB[i][:, 0:KVR],
                func=ACT.Square,
                scale=1.0 / math.sqrt(KVR),
                accum_out=MK[c][:, k : k + 1],
            )

        def sqrt_k(i):
            (c, k, n) = GROUP[i]
            if k == n - 1:
                sk = ring3.tile([P, CH], F32, name="sk", tag="sk")
                nc.scalar.activation(
                    out=sk[:, 0:n],
                    in_=MK[c][:, 0:n],
                    func=ACT.Abs_reciprocal_sqrt,
                    bias=EPS,
                    scale=1.0,
                )
                SK[c] = sk

        def nope_on_scalar(i):
            return i >= NOPE_ON_SCALAR_FROM or i % 4 == 1

        def get_oc(c):
            if c not in OC:
                oc = ring3.tile([P, CH, 512], F32, name="oc", tag="oc")
                OC[c] = oc
            return OC[c]

        def ev(i):
            (c, k, n) = GROUP[i]
            if k == 0:
                pr = ring2.tile([P, CH, 3, 2, 2, 32], F32, name="pr", tag="pr")
                PR[c] = pr
            oc, pr, ob = get_oc(c), PR[c], OB[i]
            nc.vector.tensor_tensor(
                out=pr[:, k].rearrange("p g x y j -> p g x (y j)"),
                in0=ob[:, 64:256]
                .rearrange("p (g c) -> p g c", g=3)
                .unsqueeze(2)
                .to_broadcast([P, 3, 2, 64]),
                in1=tab[:, i]
                .rearrange("p x y j -> p x (y j)")
                .unsqueeze(1)
                .to_broadcast([P, 3, 2, 64]),
                op=ALU.mult,
            )
            nc.vector.tensor_tensor(
                out=oc[:, k, 384:448], in0=ob[:, 0:KVR], in1=gamk[:], op=ALU.mult
            )
            add_eng = nc.vector if i == NT - 1 else nc.gpsimd
            add_eng.tensor_tensor(
                out=oc[:, k, 0:384]
                .rearrange("p (h c) -> p h c", h=2)[:, :, 128:192]
                .rearrange("p h (x j) -> p h x j", x=2),
                in0=pr[:, k, 1:3, :, 0, :],
                in1=pr[:, k, 1:3, :, 1, :],
                op=ALU.add,
            )
            add_eng.tensor_tensor(
                out=oc[:, k, 448:512].rearrange("p (x j) -> p x j", x=2),
                in0=pr[:, k, 0, :, 0, :],
                in1=pr[:, k, 0, :, 1, :],
                op=ALU.add,
            )

        def ev_nope(i, on_scalar):
            if nope_on_scalar(i) != on_scalar:
                return
            (c, k, n) = GROUP[i]
            dst = get_oc(c)[:, k, 0:384].rearrange("p (h c) -> p h c", h=2)[:, :, 0:128]
            src = OB[i][:, 256:512].rearrange("p (h c) -> p h c", h=2)
            if on_scalar:
                nc.scalar.copy(out=dst, in_=src)
            else:
                nc.vector.tensor_copy(out=dst, in_=src)

        def ev_fin(i):
            (c, k, n) = GROUP[i]
            oc = OC[c]
            if k == n - 1:
                fin_eng = nc.vector if i == NT - 1 else nc.gpsimd
                fin_eng.tensor_tensor(
                    out=oc[:, 0:n, 384:448],
                    in0=oc[:, 0:n, 384:448],
                    in1=SK[c][:, 0:n].unsqueeze(2).to_broadcast([P, n, KVR]),
                    op=ALU.mult,
                )
                nc.sync.dma_start(out=out_v[:, i - n + 1 : i + 1, :], in_=oc[:, 0:n, :])

        for s in range(NT + L_EV + 1):
            if ok(s):
                t1(s)
            if ok(s - L_T2):
                t2(s - L_T2)
            if s == 1:
                prep_gamma_mm()
            if ok(s - L_EV):
                ev_nope(s - L_EV, True)
            if ok(s):
                c1(s)
            if ok(s - L_M1 - 1):
                sqrt_a(s - L_M1 - 1)
            if ok(s - L_M2 - 1):
                sqrt_k(s - L_M2 - 1)
            if ok(s - L_T2):
                c2(s - L_T2)
            if ok(s - L_CQ):
                cqf(s - L_CQ)
            if ok(s - L_Q1):
                q1(s - L_Q1)
            if ok(s - L_Q2):
                q2(s - L_Q2)
            if ok(s - L_EV):
                ev(s - L_EV)
            if ok(s - L_EV):
                ev_nope(s - L_EV, False)
                ev_fin(s - L_EV)
            if s < 3:
                prep_w_regroup(s)
            if s == 3:
                prep_w_quant()
            if s == 6:
                make_tab()
            if ok(s - L_M1):
                m1(s - L_M1)
            if ok(s - L_M2):
                m2(s - L_M2)
            if ok(s - L_M1):
                sq(s - L_M1)
            if ok(s - L_M2):
                sqk(s - L_M2)
